import numpy as np
import ml_dtypes


def mxq(x, axis, fmt="e4m3"):
    dtype, down = {"e4m3": (ml_dtypes.float8_e4m3fn, 7), "e5m2": (ml_dtypes.float8_e5m2, 14)}[fmt]
    v = np.moveaxis(np.asarray(x, np.float32).astype(ml_dtypes.bfloat16).astype(np.float64), axis, -1)
    blocks = v.reshape(v.shape[:-1] + (-1, 32))
    amax = np.abs(blocks).max(-1, keepdims=True)
    byte = np.maximum(np.where(amax > 0, np.frexp(amax)[1] - 1 + 127, 0) - down, 1)
    scale = np.exp2(byte - 127.0)
    codes = (blocks / scale).astype(np.float32).astype(dtype).astype(np.float64)
    return np.moveaxis((codes * scale).reshape(v.shape), -1, axis)


WIDE = False


def mx_kscale(k):
    if not WIDE:
        return np.ones(k)
    levels = np.array([10, -10, 5, -5, 0])
    a = np.random.permutation(np.resize(levels, k // 512 * 4)).reshape(k // 512, 4)
    idx = np.arange(k)
    return np.exp2(a[idx // 512, idx % 128 // 32])


BF16 = ml_dtypes.bfloat16


def bf(x):
    return np.asarray(x, np.float32).astype(BF16)


def f64(x):
    return np.asarray(x).astype(np.float64)


B, T, D, E, F = 4, 1024, 1024, 256, 4096
EPS = 1e-6


def rms_norm(x, w):
    rms = np.sqrt(np.mean(x * x, axis=-1, keepdims=True) + EPS)
    return x / rms * w


def setup_inputs():
    s = mx_kscale(D)
    return {"x": bf(np.random.standard_normal((B, T, D))),
            "attn_norm_w": bf((1.0 + 0.1 * np.random.standard_normal(D)) * s),
            "wq": bf(np.random.standard_normal((D, E)) * 1.5 / np.sqrt(D) / s[:, None]),
            "bq": bf(np.random.standard_normal(E) * 0.1),
            "wk": bf(np.random.standard_normal((D, E)) * 1.5 / np.sqrt(D) / s[:, None]),
            "bk": bf(np.random.standard_normal(E) * 0.1),
            "wv": bf(np.random.standard_normal((D, E)) / np.sqrt(D) / s[:, None]),
            "bv": bf(np.random.standard_normal(E) * 0.1)}


def reference(x, attn_norm_w, wq, bq, wk, bk, wv, bv):
    xn = mxq(rms_norm(f64(x), f64(attn_norm_w)), 2, "e4m3")
    q = (xn @ mxq(f64(wq), 0, "e4m3")) + f64(bq)
    k = (xn @ mxq(f64(wk), 0, "e4m3")) + f64(bk)
    v = (xn @ mxq(f64(wv), 0, "e4m3")) + f64(bv)
    return q, k, v

@@ -1,0 +1,227 @@
+from contextlib import ExitStack
+
+import concourse.mybir as mybir
+from concourse.masks import make_identity
+
+F32 = mybir.dt.float32
+BF16 = mybir.dt.bfloat16
+I32 = mybir.dt.int32
+U32 = mybir.dt.uint32
+U8 = mybir.dt.uint8
+FP8X4 = mybir.dt.float8_e4m3fn_x4
+ACT = mybir.ActivationFunctionType
+ALU = mybir.AluOpType
+
+P = 128
+PACK = 4
+PAIR = 2
+K_PASS = P * PACK
+TOKENS = 4 * 1024
+D = 1024
+E = 256
+PROJ = 3
+PASSES = D // K_PASS
+HALVES = D // (P * PAIR)
+TILES = 2
+UNIT = TILES * P
+UNITS = TOKENS // UNIT
+BANK = 512
+EPS = 1e-6
+
+FLOPS = 2 * TOKENS * D * PROJ * E
+
+
+def tile_tinyblock_pa_t_kernel(
+    tc, x, attn_norm_w, wq, bq, wk, bk, wv, bv, out_0, out_1, out_2
+):
+    nc = tc.nc
+    x_rows = x.flatten_outer_dims()
+    out_rows = [out_0.flatten_outer_dims(), out_1.flatten_outer_dims(), out_2.flatten_outer_dims()]
+    weights = [wq, wk, wv]
+    biases = [bq, bk, bv]
+
+    with ExitStack() as ctx:
+        ctx.enter_context(tc.manual_schedule())
+        const = ctx.enter_context(tc.tile_pool(name="const", bufs=1))
+        x_pool = ctx.enter_context(tc.tile_pool(name="x", bufs=UNITS))
+        small = ctx.enter_context(tc.tile_pool(name="small", bufs=3))
+        work = ctx.enter_context(tc.tile_pool(name="work", bufs=2))
+        store = ctx.enter_context(tc.tile_pool(name="store", bufs=3))
+        psum_t = ctx.enter_context(tc.psum_pool(name="psum_t", bufs=3))
+        psum_o = ctx.enter_context(tc.psum_pool(name="psum_o", bufs=1))
+
+        vector_row = const.tile([1, D + PROJ * E], BF16)
+        nc.scalar.dma_start(out=vector_row[:, 0:D], in_=attn_norm_w.unsqueeze(0))
+        for i in range(PROJ):
+            nc.scalar.dma_start(
+                out=vector_row[:, D + i * E : D + (i + 1) * E], in_=biases[i].unsqueeze(0)
+            )
+
+        w_raw = const.tile([P, PROJ, PASSES * PACK, E], BF16)
+
+        def load_weight(i):
+            nc.sync.dma_start(
+                out=w_raw[:, i].rearrange("p (h e) n -> p h (e n)", e=PAIR),
+                in_=weights[i].rearrange("(h p e) n -> p h (e n)", p=P, e=PAIR),
+            )
+
+        x_units = []
+
+        def load_unit(u):
+            x_unit = x_pool.tile([P, TILES, D], BF16, name="x_unit")
+            nc.sync.dma_start(
+                out=x_unit[:],
+                in_=x_rows[u * UNIT : (u + 1) * UNIT, :].rearrange("(p j) f -> p j f", j=TILES),
+            )
+            x_units.append(x_unit)
+
+        load_weight(0)
+        load_unit(0)
+        for i in range(1, PROJ):
+            load_weight(i)
+        for u in range(1, UNITS):
+            load_unit(u)
+
+        eps = const.tile([P, 1], F32)
+        nc.vector.memset(eps[:], EPS)
+        vectors = const.tile([P, D + PROJ * E], BF16)
+        nc.vector.memset(vectors[:].bitcast(I32), 0)
+        nc.vector.tensor_copy(out=vectors[0:1, :], in_=vector_row[:])
+        ones = const.tile([P, P], BF16)
+        nc.vector.memset(ones[:], 1.0)
+        ident = const.tile([P, P], F32)
+        make_identity(nc, ident[:])
+
+        warm = const.tile([P, 1], F32)
+        nc.scalar.activation(out=warm[:], in_=eps[:], func=ACT.Abs_reciprocal_sqrt)
+
+        gain = const.tile([P, D], BF16)
+        bias = const.tile([P, PROJ, E], F32)
+        for h in range(D // BANK):
+            spread = psum_t.tile([P, BANK], F32, tag="xt")
+            nc.tensor.matmul(
+                out=spread[:], lhsT=ones[:], rhs=vectors[:, h * BANK : (h + 1) * BANK],
+                start=True, stop=True,
+            )
+            nc.scalar.copy(out=gain[:, h * BANK : (h + 1) * BANK], in_=spread[:])
+        for i in range(PROJ):
+            spread = psum_t.tile([P, E], F32, tag="xt")
+            nc.tensor.matmul(
+                out=spread[:], lhsT=ones[:], rhs=vectors[:, D + i * E : D + (i + 1) * E],
+                start=True, stop=True,
+            )
+            nc.scalar.copy(out=bias[:, i, :], in_=spread[:])
+
+        w_grouped = const.tile([P, PROJ, PASSES, E, PACK], BF16, align_bytes=64)
+        w_codes = const.tile([P, PROJ, PASSES, E], U32, align_bytes=64)
+        w_scales = const.tile([P, PROJ, PASSES, E], U8, align_bytes=64)
+
+        def group_weight(i):
+            nc.vector.tensor_copy(
+                out=w_grouped[:, i],
+                in_=w_raw[:, i].rearrange("p (c t) n -> p c n t", t=PACK),
+            )
+
+        def quantise_weight(i):
+            nc.vector.quantize_mx(
+                out=w_codes[:, i].rearrange("p c n -> p (c n)").bitcast(FP8X4),
+                scales=w_scales[:, i].rearrange("p c n -> p (c n)"),
+                in_=w_grouped[:, i].rearrange("p c n t -> p (c n t)"),
+            )
+
+        group_weight(0)
+        for i in range(1, PROJ):
+            group_weight(i)
+            quantise_weight(i - 1)
+        quantise_weight(PROJ - 1)
+
+        rinv_of = {}
+        grouped_of = {}
+        acc_of = {}
+
+        def statistics(u):
+            sumsq = small.tile([P, TILES], F32, name="sumsq")
+            for j in range(TILES):
+                squares = work.tile([P, D], BF16, name="squares")
+                nc.scalar.activation(
+                    out=squares[:], in_=x_units[u][:, j, :], func=ACT.Square,
+                    accum_out=sumsq[:, j : j + 1],
+                )
+            rinv = small.tile([P, TILES], F32, name="rinv")
+            nc.scalar.activation(
+                out=rinv[:], in_=sumsq[:], func=ACT.Abs_reciprocal_sqrt, scale=1.0 / D, bias=eps[:]
+            )
+            rinv_of[u] = rinv
+
+        def normalise_and_transpose(u):
+            xn = work.tile([P, TILES, D], BF16, name="xn")
+            grouped = work.tile([P, TILES, PASSES, P, PACK], BF16, name="grouped", align_bytes=64)
+            for j in range(TILES):
+                nc.vector.scalar_tensor_tensor(
+                    out=xn[:, j, :], in0=x_units[u][:, j, :], scalar=rinv_of[u][:, j : j + 1],
+                    in1=gain[:], op0=ALU.mult, op1=ALU.mult,
+                )
+                xn_words = xn[:, j, :].bitcast(F32)
+                xt = psum_t.tile([P, HALVES, P], F32, name="xt")
+                for h in range(HALVES):
+                    nc.tensor.transpose(
+                        out=xt[:, h, :], in_=xn_words[:, h * P : (h + 1) * P], identity=ident[:]
+                    )
+                nc.scalar.copy(
+                    out=grouped[:, j]
+                    .rearrange("p c r t -> p (c r t)")
+                    .bitcast(F32)
+                    .rearrange("p (c r u) -> p c r u", c=PASSES, u=PAIR),
+                    in_=xt[:].rearrange("p (c u) r -> p c r u", u=PAIR),
+                )
+            grouped_of[u] = grouped
+
+        def quantise_and_project(u):
+            codes = work.tile([P, TILES, PASSES, P], U32, name="codes", align_bytes=64)
+            scales = work.tile([P, TILES, PASSES, P], U8, name="scales", align_bytes=64)
+            nc.vector.quantize_mx(
+                out=codes[:].rearrange("p j c r -> p (j c r)").bitcast(FP8X4),
+                scales=scales[:].rearrange("p j c r -> p (j c r)"),
+                in_=grouped_of[u][:].rearrange("p j c r t -> p (j c r t)"),
+            )
+            acc_of[u] = []
+            for i in range(PROJ):
+                acc = psum_o.tile([P, TILES, E], F32, name="acc%d" % i)
+                for j in range(TILES):
+                    for c in range(PASSES):
+                        nc.tensor.matmul_mx(
+                            out=acc[:, j, :],
+                            lhsT=codes[:, j, c, :].bitcast(FP8X4),
+                            lhsT_scale=scales[:, j, c, :],
+                            rhs=w_codes[:, i, c, :].bitcast(FP8X4),
+                            rhs_scale=w_scales[:, i, c, :],
+                            start=(c == 0),
+                            stop=(c == PASSES - 1),
+                        )
+                acc_of[u].append(acc)
+
+        def add_bias_and_store(u):
+            accs = acc_of[u]
+            result = store.tile([P, PROJ, TILES, E], F32, name="result")
+            for i in range(PROJ):
+                nc.vector.tensor_tensor(
+                    out=result[:, i], in0=accs[i][:],
+                    in1=bias[:, i, :].unsqueeze(1).to_broadcast([P, TILES, E]), op=ALU.add,
+                )
+                nc.sync.dma_start(
+                    out=out_rows[i][u * UNIT : (u + 1) * UNIT, :].rearrange(
+                        "(p j) e -> p j e", j=TILES
+                    ),
+                    in_=result[:, i],
+                )
+
+        STAGES = 4
+        for step in range(UNITS + STAGES - 1):
+            if step < UNITS:
+                statistics(step)
+            if 0 <= step - 1 < UNITS:
+                normalise_and_transpose(step - 1)
+            if 0 <= step - 3 < UNITS:
+                add_bias_and_store(step - 3)
+            if 0 <= step - 2 < UNITS:
+                quantise_and_project(step - 2)

@@ -27,6 +27,7 @@ UNIT = TILES * P
 UNITS = TOKENS // UNIT
 BANK = 512
 EPS = 1e-6
+GPSIMD_EVERY = 2
 
 FLOPS = 2 * TOKENS * D * PROJ * E
 
@@ -51,9 +52,9 @@ def tile_tinyblock_pa_t_kernel(
         psum_o = ctx.enter_context(tc.psum_pool(name="psum_o", bufs=1))
 
         vector_row = const.tile([1, D + PROJ * E], BF16)
-        nc.scalar.dma_start(out=vector_row[:, 0:D], in_=attn_norm_w.unsqueeze(0))
+        nc.sync.dma_start(out=vector_row[:, 0:D], in_=attn_norm_w.unsqueeze(0))
         for i in range(PROJ):
-            nc.scalar.dma_start(
+            nc.sync.dma_start(
                 out=vector_row[:, D + i * E : D + (i + 1) * E], in_=biases[i].unsqueeze(0)
             )
 
@@ -95,15 +96,15 @@ def tile_tinyblock_pa_t_kernel(
         warm = const.tile([P, 1], F32)
         nc.scalar.activation(out=warm[:], in_=eps[:], func=ACT.Abs_reciprocal_sqrt)
 
-        gain = const.tile([P, D], BF16)
+        gain_psum = psum_o.tile([P, D], BF16)
+        gain_sbuf = const.tile([P, D], BF16)
         bias = const.tile([P, PROJ, E], F32)
         for h in range(D // BANK):
-            spread = psum_t.tile([P, BANK], F32, tag="xt")
             nc.tensor.matmul(
-                out=spread[:], lhsT=ones[:], rhs=vectors[:, h * BANK : (h + 1) * BANK],
-                start=True, stop=True,
+                out=gain_psum[:, h * BANK : (h + 1) * BANK], lhsT=ones[:],
+                rhs=vectors[:, h * BANK : (h + 1) * BANK], start=True, stop=True,
             )
-            nc.scalar.copy(out=gain[:, h * BANK : (h + 1) * BANK], in_=spread[:])
+        nc.scalar.copy(out=gain_sbuf[:], in_=gain_psum[:])
         for i in range(PROJ):
             spread = psum_t.tile([P, E], F32, tag="xt")
             nc.tensor.matmul(
@@ -157,10 +158,21 @@ def tile_tinyblock_pa_t_kernel(
             xn = work.tile([P, TILES, D], BF16, name="xn")
             grouped = work.tile([P, TILES, PASSES, P, PACK], BF16, name="grouped", align_bytes=64)
             for j in range(TILES):
-                nc.vector.scalar_tensor_tensor(
-                    out=xn[:, j, :], in0=x_units[u][:, j, :], scalar=rinv_of[u][:, j : j + 1],
-                    in1=gain[:], op0=ALU.mult, op1=ALU.mult,
-                )
+                rinv = rinv_of[u][:, j : j + 1]
+                if (u * TILES + j) % GPSIMD_EVERY == GPSIMD_EVERY - 1:
+                    scaled = work.tile([P, D], F32, name="scaled")
+                    nc.gpsimd.tensor_scalar(
+                        out=scaled[:], in0=x_units[u][:, j, :], scalar1=rinv, scalar2=1.0,
+                        op0=ALU.mult, op1=ALU.mult,
+                    )
+                    nc.gpsimd.tensor_tensor(
+                        out=xn[:, j, :], in0=scaled[:], in1=gain_sbuf[:], op=ALU.mult
+                    )
+                else:
+                    nc.vector.scalar_tensor_tensor(
+                        out=xn[:, j, :], in0=x_units[u][:, j, :], scalar=rinv,
+                        in1=gain_psum[:], op0=ALU.mult, op1=ALU.mult,
+                    )
                 xn_words = xn[:, j, :].bitcast(F32)
                 xt = psum_t.tile([P, HALVES, P], F32, name="xt")
                 for h in range(HALVES):

@@ -27,7 +27,7 @@ UNIT = TILES * P
 UNITS = TOKENS // UNIT
 BANK = 512
 EPS = 1e-6
-GPSIMD_EVERY = 2
+GPSIMD_EVERY = 3
 
 FLOPS = 2 * TOKENS * D * PROJ * E
 

@@ -25,7 +25,11 @@ HALVES = D // (P * PAIR)
 TILES = 2
 UNIT = TILES * P
 UNITS = TOKENS // UNIT
+ALL_TILES = TOKENS // P
 BANK = 512
+PER_BANK = BANK // E
+OUT_BANKS = -(-PROJ // PER_BANK)
+LEAD = 4
 EPS = 1e-6
 GPSIMD_EVERY = 3
 
@@ -45,11 +49,13 @@ def tile_tinyblock_pa_t_kernel(
         ctx.enter_context(tc.manual_schedule())
         const = ctx.enter_context(tc.tile_pool(name="const", bufs=1))
         x_pool = ctx.enter_context(tc.tile_pool(name="x", bufs=UNITS))
-        small = ctx.enter_context(tc.tile_pool(name="small", bufs=3))
-        work = ctx.enter_context(tc.tile_pool(name="work", bufs=2))
+        small = ctx.enter_context(tc.tile_pool(name="small", bufs=LEAD + 2))
+        normed = ctx.enter_context(tc.tile_pool(name="normed", bufs=LEAD + 2))
+        work = ctx.enter_context(tc.tile_pool(name="work", bufs=3))
         store = ctx.enter_context(tc.tile_pool(name="store", bufs=3))
+        psum_g = ctx.enter_context(tc.psum_pool(name="psum_g", bufs=1))
         psum_t = ctx.enter_context(tc.psum_pool(name="psum_t", bufs=3))
-        psum_o = ctx.enter_context(tc.psum_pool(name="psum_o", bufs=1))
+        psum_o = ctx.enter_context(tc.psum_pool(name="psum_o", bufs=2))
 
         vector_row = const.tile([1, D + PROJ * E], BF16)
         nc.sync.dma_start(out=vector_row[:, 0:D], in_=attn_norm_w.unsqueeze(0))
@@ -96,7 +102,7 @@ def tile_tinyblock_pa_t_kernel(
         warm = const.tile([P, 1], F32)
         nc.scalar.activation(out=warm[:], in_=eps[:], func=ACT.Abs_reciprocal_sqrt)
 
-        gain_psum = psum_o.tile([P, D], BF16)
+        gain_psum = psum_g.tile([P, D], BF16)
         gain_sbuf = const.tile([P, D], BF16)
         bias = const.tile([P, PROJ, E], F32)
         for h in range(D // BANK):
@@ -136,104 +142,136 @@ def tile_tinyblock_pa_t_kernel(
             quantise_weight(i - 1)
         quantise_weight(PROJ - 1)
 
+        sumsq_of = {}
         rinv_of = {}
+        xn_of = {}
+        xt_of = {}
         grouped_of = {}
+        codes_of = {}
+        scales_of = {}
         acc_of = {}
+        result_of = {}
 
-        def statistics(u):
-            sumsq = small.tile([P, TILES], F32, name="sumsq")
-            for j in range(TILES):
-                squares = work.tile([P, D], BF16, name="squares")
-                nc.scalar.activation(
-                    out=squares[:], in_=x_units[u][:, j, :], func=ACT.Square,
-                    accum_out=sumsq[:, j : j + 1],
-                )
-            rinv = small.tile([P, TILES], F32, name="rinv")
+        def statistics(n):
+            u, j = divmod(n, TILES)
+            if j == 0:
+                sumsq = small.tile([P, TILES], F32, name="sumsq")
+                sumsq_of[u] = sumsq
+            squares = work.tile([P, D], BF16, name="squares")
             nc.scalar.activation(
-                out=rinv[:], in_=sumsq[:], func=ACT.Abs_reciprocal_sqrt, scale=1.0 / D, bias=eps[:]
+                out=squares[:], in_=x_units[u][:, j, :], func=ACT.Square,
+                accum_out=sumsq_of[u][:, j : j + 1],
             )
-            rinv_of[u] = rinv
-
-        def normalise_and_transpose(u):
-            xn = work.tile([P, TILES, D], BF16, name="xn")
-            grouped = work.tile([P, TILES, PASSES, P, PACK], BF16, name="grouped", align_bytes=64)
-            for j in range(TILES):
-                rinv = rinv_of[u][:, j : j + 1]
-                if (u * TILES + j) % GPSIMD_EVERY == GPSIMD_EVERY - 1:
-                    scaled = work.tile([P, D], F32, name="scaled")
-                    nc.gpsimd.tensor_scalar(
-                        out=scaled[:], in0=x_units[u][:, j, :], scalar1=rinv, scalar2=1.0,
-                        op0=ALU.mult, op1=ALU.mult,
-                    )
-                    nc.gpsimd.tensor_tensor(
-                        out=xn[:, j, :], in0=scaled[:], in1=gain_sbuf[:], op=ALU.mult
-                    )
-                else:
-                    nc.vector.scalar_tensor_tensor(
-                        out=xn[:, j, :], in0=x_units[u][:, j, :], scalar=rinv,
-                        in1=gain_psum[:], op0=ALU.mult, op1=ALU.mult,
-                    )
-                xn_words = xn[:, j, :].bitcast(F32)
-                xt = psum_t.tile([P, HALVES, P], F32, name="xt")
-                for h in range(HALVES):
-                    nc.tensor.transpose(
-                        out=xt[:, h, :], in_=xn_words[:, h * P : (h + 1) * P], identity=ident[:]
-                    )
-                nc.scalar.copy(
-                    out=grouped[:, j]
-                    .rearrange("p c r t -> p (c r t)")
-                    .bitcast(F32)
-                    .rearrange("p (c r u) -> p c r u", c=PASSES, u=PAIR),
-                    in_=xt[:].rearrange("p (c u) r -> p c r u", u=PAIR),
+            if j == TILES - 1:
+                rinv = small.tile([P, TILES], F32, name="rinv")
+                nc.scalar.activation(
+                    out=rinv[:], in_=sumsq_of[u][:], func=ACT.Abs_reciprocal_sqrt,
+                    scale=1.0 / D, bias=eps[:],
                 )
-            grouped_of[u] = grouped
+                rinv_of[u] = rinv
 
-        def quantise_and_project(u):
-            codes = work.tile([P, TILES, PASSES, P], U32, name="codes", align_bytes=64)
-            scales = work.tile([P, TILES, PASSES, P], U8, name="scales", align_bytes=64)
+        def normalise(n):
+            u, j = divmod(n, TILES)
+            rinv = rinv_of[u][:, j : j + 1]
+            xn = normed.tile([P, D], BF16, name="xn")
+            if n % GPSIMD_EVERY == GPSIMD_EVERY - 1:
+                scaled = work.tile([P, D], F32, name="scaled")
+                nc.gpsimd.tensor_scalar(
+                    out=scaled[:], in0=x_units[u][:, j, :], scalar1=rinv, scalar2=1.0,
+                    op0=ALU.mult, op1=ALU.mult,
+                )
+                nc.gpsimd.tensor_tensor(out=xn[:], in0=scaled[:], in1=gain_sbuf[:], op=ALU.mult)
+            else:
+                nc.vector.scalar_tensor_tensor(
+                    out=xn[:], in0=x_units[u][:, j, :], scalar=rinv, in1=gain_psum[:],
+                    op0=ALU.mult, op1=ALU.mult,
+                )
+            xn_of[n] = xn
+
+        def transpose(n):
+            xn_words = xn_of[n][:].bitcast(F32)
+            xt = psum_t.tile([P, HALVES, P], F32, name="xt")
+            for h in range(HALVES):
+                nc.tensor.transpose(
+                    out=xt[:, h, :], in_=xn_words[:, h * P : (h + 1) * P], identity=ident[:]
+                )
+            xt_of[n] = xt
+
+        def copy_out(n):
+            grouped = work.tile([P, PASSES, P, PACK], BF16, name="grouped", align_bytes=64)
+            nc.scalar.copy(
+                out=grouped[:]
+                .rearrange("p c r t -> p (c r t)")
+                .bitcast(F32)
+                .rearrange("p (c r u) -> p c r u", c=PASSES, u=PAIR),
+                in_=xt_of[n][:].rearrange("p (c u) r -> p c r u", u=PAIR),
+            )
+            grouped_of[n] = grouped
+
+        def quantise(n):
+            codes = work.tile([P, PASSES, P], U32, name="codes", align_bytes=64)
+            scales = work.tile([P, PASSES, P], U8, name="scales", align_bytes=64)
             nc.vector.quantize_mx(
-                out=codes[:].rearrange("p j c r -> p (j c r)").bitcast(FP8X4),
-                scales=scales[:].rearrange("p j c r -> p (j c r)"),
-                in_=grouped_of[u][:].rearrange("p j c r t -> p (j c r t)"),
+                out=codes[:].rearrange("p c r -> p (c r)").bitcast(FP8X4),
+                scales=scales[:].rearrange("p c r -> p (c r)"),
+                in_=grouped_of[n][:].rearrange("p c r t -> p (c r t)"),
             )
-            acc_of[u] = []
-            for i in range(PROJ):
-                acc = psum_o.tile([P, TILES, E], F32, name="acc%d" % i)
-                for j in range(TILES):
-                    for c in range(PASSES):
-                        nc.tensor.matmul_mx(
-                            out=acc[:, j, :],
-                            lhsT=codes[:, j, c, :].bitcast(FP8X4),
-                            lhsT_scale=scales[:, j, c, :],
-                            rhs=w_codes[:, i, c, :].bitcast(FP8X4),
-                            rhs_scale=w_scales[:, i, c, :],
-                            start=(c == 0),
-                            stop=(c == PASSES - 1),
-                        )
-                acc_of[u].append(acc)
+            codes_of[n] = codes
+            scales_of[n] = scales
 
-        def add_bias_and_store(u):
-            accs = acc_of[u]
-            result = store.tile([P, PROJ, TILES, E], F32, name="result")
+        def project(n):
+            acc_of[n] = []
+            for b in range(OUT_BANKS):
+                acc = psum_o.tile([P, PER_BANK, E], F32, name="acc%d" % b)
+                acc_of[n].append(acc)
             for i in range(PROJ):
+                for c in range(PASSES):
+                    nc.tensor.matmul_mx(
+                        out=acc_of[n][i // PER_BANK][:, i % PER_BANK, :],
+                        lhsT=codes_of[n][:, c, :].bitcast(FP8X4),
+                        lhsT_scale=scales_of[n][:, c, :],
+                        rhs=w_codes[:, i, c, :].bitcast(FP8X4),
+                        rhs_scale=w_scales[:, i, c, :],
+                        start=(c == 0),
+                        stop=(c == PASSES - 1),
+                    )
+
+        def add_bias_and_store(n):
+            u, j = divmod(n, TILES)
+            if j == 0:
+                result = store.tile([P, PROJ, TILES, E], F32, name="result")
+                result_of[u] = result
+            for b in range(OUT_BANKS):
+                first = b * PER_BANK
+                last = min(PROJ, first + PER_BANK)
                 nc.vector.tensor_tensor(
-                    out=result[:, i], in0=accs[i][:],
-                    in1=bias[:, i, :].unsqueeze(1).to_broadcast([P, TILES, E]), op=ALU.add,
+                    out=result_of[u][:, first:last, j, :],
+                    in0=acc_of[n][b][:, 0 : last - first, :],
+                    in1=bias[:, first:last, :],
+                    op=ALU.add,
                 )
-                nc.sync.dma_start(
-                    out=out_rows[i][u * UNIT : (u + 1) * UNIT, :].rearrange(
-                        "(p j) e -> p j e", j=TILES
-                    ),
-                    in_=result[:, i],
-                )
+            if j == TILES - 1:
+                for i in range(PROJ):
+                    nc.sync.dma_start(
+                        out=out_rows[i][u * UNIT : (u + 1) * UNIT, :].rearrange(
+                            "(p j) e -> p j e", j=TILES
+                        ),
+                        in_=result_of[u][:, i],
+                    )
 
-        STAGES = 4
-        for step in range(UNITS + STAGES - 1):
-            if step < UNITS:
-                statistics(step)
-            if 0 <= step - 1 < UNITS:
-                normalise_and_transpose(step - 1)
-            if 0 <= step - 3 < UNITS:
+        for n in range(LEAD):
+            statistics(n)
+        for step in range(ALL_TILES + 3):
+            if 0 <= step - 1 < ALL_TILES:
+                copy_out(step - 1)
+            if step + LEAD < ALL_TILES:
+                statistics(step + LEAD)
+            if 0 <= step - 2 < ALL_TILES:
+                project(step - 2)
+            if step < ALL_TILES:
+                normalise(step)
+                transpose(step)
+            if 0 <= step - 3 < ALL_TILES:
                 add_bias_and_store(step - 3)
-            if 0 <= step - 2 < UNITS:
-                quantise_and_project(step - 2)
+            if 0 <= step - 1 < ALL_TILES:
+                quantise(step - 1)

@@ -198,28 +198,33 @@ def tile_tinyblock_pa_t_kernel(
             xt_of[n] = xt
 
         def copy_out(n):
-            grouped = work.tile([P, PASSES, P, PACK], BF16, name="grouped", align_bytes=64)
+            u, j = divmod(n, TILES)
+            if j == 0:
+                grouped = work.tile(
+                    [P, TILES, PASSES, P, PACK], BF16, name="grouped", align_bytes=64
+                )
+                grouped_of[u] = grouped
             nc.scalar.copy(
-                out=grouped[:]
+                out=grouped_of[u][:, j]
                 .rearrange("p c r t -> p (c r t)")
                 .bitcast(F32)
                 .rearrange("p (c r u) -> p c r u", c=PASSES, u=PAIR),
                 in_=xt_of[n][:].rearrange("p (c u) r -> p c r u", u=PAIR),
             )
-            grouped_of[n] = grouped
 
-        def quantise(n):
-            codes = work.tile([P, PASSES, P], U32, name="codes", align_bytes=64)
-            scales = work.tile([P, PASSES, P], U8, name="scales", align_bytes=64)
+        def quantise(u):
+            codes = work.tile([P, TILES, PASSES, P], U32, name="codes", align_bytes=64)
+            scales = work.tile([P, TILES, PASSES, P], U8, name="scales", align_bytes=64)
             nc.vector.quantize_mx(
-                out=codes[:].rearrange("p c r -> p (c r)").bitcast(FP8X4),
-                scales=scales[:].rearrange("p c r -> p (c r)"),
-                in_=grouped_of[n][:].rearrange("p c r t -> p (c r t)"),
+                out=codes[:].rearrange("p j c r -> p (j c r)").bitcast(FP8X4),
+                scales=scales[:].rearrange("p j c r -> p (j c r)"),
+                in_=grouped_of[u][:].rearrange("p j c r t -> p (j c r t)"),
             )
-            codes_of[n] = codes
-            scales_of[n] = scales
+            codes_of[u] = codes
+            scales_of[u] = scales
 
         def project(n):
+            u, j = divmod(n, TILES)
             acc_of[n] = []
             for b in range(OUT_BANKS):
                 acc = psum_o.tile([P, PER_BANK, E], F32, name="acc%d" % b)
@@ -228,8 +233,8 @@ def tile_tinyblock_pa_t_kernel(
                 for c in range(PASSES):
                     nc.tensor.matmul_mx(
                         out=acc_of[n][i // PER_BANK][:, i % PER_BANK, :],
-                        lhsT=codes_of[n][:, c, :].bitcast(FP8X4),
-                        lhsT_scale=scales_of[n][:, c, :],
+                        lhsT=codes_of[u][:, j, c, :].bitcast(FP8X4),
+                        lhsT_scale=scales_of[u][:, j, c, :],
                         rhs=w_codes[:, i, c, :].bitcast(FP8X4),
                         rhs_scale=w_scales[:, i, c, :],
                         start=(c == 0),
@@ -261,17 +266,17 @@ def tile_tinyblock_pa_t_kernel(
 
         for n in range(LEAD):
             statistics(n)
-        for step in range(ALL_TILES + 3):
+        for step in range(ALL_TILES + 4):
             if 0 <= step - 1 < ALL_TILES:
                 copy_out(step - 1)
             if step + LEAD < ALL_TILES:
                 statistics(step + LEAD)
-            if 0 <= step - 2 < ALL_TILES:
-                project(step - 2)
+            if 0 <= step - 3 < ALL_TILES:
+                project(step - 3)
             if step < ALL_TILES:
                 normalise(step)
                 transpose(step)
-            if 0 <= step - 3 < ALL_TILES:
-                add_bias_and_store(step - 3)
-            if 0 <= step - 1 < ALL_TILES:
-                quantise(step - 1)
+            if 0 <= step - 4 < ALL_TILES:
+                add_bias_and_store(step - 4)
+            if 0 <= step - 1 < ALL_TILES and (step - 1) % TILES == TILES - 1:
+                quantise((step - 1) // TILES)

@@ -31,7 +31,6 @@ PER_BANK = BANK // E
 OUT_BANKS = -(-PROJ // PER_BANK)
 LEAD = 4
 EPS = 1e-6
-GPSIMD_EVERY = 3
 
 FLOPS = 2 * TOKENS * D * PROJ * E
 
@@ -53,8 +52,7 @@ def tile_tinyblock_pa_t_kernel(
         normed = ctx.enter_context(tc.tile_pool(name="normed", bufs=LEAD + 2))
         work = ctx.enter_context(tc.tile_pool(name="work", bufs=3))
         store = ctx.enter_context(tc.tile_pool(name="store", bufs=3))
-        psum_g = ctx.enter_context(tc.psum_pool(name="psum_g", bufs=1))
-        psum_t = ctx.enter_context(tc.psum_pool(name="psum_t", bufs=3))
+        psum_t = ctx.enter_context(tc.psum_pool(name="psum_t", bufs=4))
         psum_o = ctx.enter_context(tc.psum_pool(name="psum_o", bufs=2))
 
         vector_row = const.tile([1, D + PROJ * E], BF16)
@@ -102,15 +100,15 @@ def tile_tinyblock_pa_t_kernel(
         warm = const.tile([P, 1], F32)
         nc.scalar.activation(out=warm[:], in_=eps[:], func=ACT.Abs_reciprocal_sqrt)
 
-        gain_psum = psum_g.tile([P, D], BF16)
-        gain_sbuf = const.tile([P, D], BF16)
+        gain = const.tile([P, D], BF16)
         bias = const.tile([P, PROJ, E], F32)
         for h in range(D // BANK):
+            spread = psum_t.tile([P, BANK], F32, tag="xt")
             nc.tensor.matmul(
-                out=gain_psum[:, h * BANK : (h + 1) * BANK], lhsT=ones[:],
-                rhs=vectors[:, h * BANK : (h + 1) * BANK], start=True, stop=True,
+                out=spread[:], lhsT=ones[:], rhs=vectors[:, h * BANK : (h + 1) * BANK],
+                start=True, stop=True,
             )
-        nc.scalar.copy(out=gain_sbuf[:], in_=gain_psum[:])
+            nc.scalar.copy(out=gain[:, h * BANK : (h + 1) * BANK], in_=spread[:])
         for i in range(PROJ):
             spread = psum_t.tile([P, E], F32, tag="xt")
             nc.tensor.matmul(
@@ -172,20 +170,11 @@ def tile_tinyblock_pa_t_kernel(
 
         def normalise(n):
             u, j = divmod(n, TILES)
-            rinv = rinv_of[u][:, j : j + 1]
             xn = normed.tile([P, D], BF16, name="xn")
-            if n % GPSIMD_EVERY == GPSIMD_EVERY - 1:
-                scaled = work.tile([P, D], F32, name="scaled")
-                nc.gpsimd.tensor_scalar(
-                    out=scaled[:], in0=x_units[u][:, j, :], scalar1=rinv, scalar2=1.0,
-                    op0=ALU.mult, op1=ALU.mult,
-                )
-                nc.gpsimd.tensor_tensor(out=xn[:], in0=scaled[:], in1=gain_sbuf[:], op=ALU.mult)
-            else:
-                nc.vector.scalar_tensor_tensor(
-                    out=xn[:], in0=x_units[u][:, j, :], scalar=rinv, in1=gain_psum[:],
-                    op0=ALU.mult, op1=ALU.mult,
-                )
+            nc.vector.scalar_tensor_tensor(
+                out=xn[:], in0=x_units[u][:, j, :], scalar=rinv_of[u][:, j : j + 1], in1=gain[:],
+                op0=ALU.mult, op1=ALU.mult,
+            )
             xn_of[n] = xn
 
         def transpose(n):
@@ -198,33 +187,28 @@ def tile_tinyblock_pa_t_kernel(
             xt_of[n] = xt
 
         def copy_out(n):
-            u, j = divmod(n, TILES)
-            if j == 0:
-                grouped = work.tile(
-                    [P, TILES, PASSES, P, PACK], BF16, name="grouped", align_bytes=64
-                )
-                grouped_of[u] = grouped
+            grouped = work.tile([P, PASSES, P, PACK], BF16, name="grouped", align_bytes=64)
             nc.scalar.copy(
-                out=grouped_of[u][:, j]
+                out=grouped[:]
                 .rearrange("p c r t -> p (c r t)")
                 .bitcast(F32)
                 .rearrange("p (c r u) -> p c r u", c=PASSES, u=PAIR),
                 in_=xt_of[n][:].rearrange("p (c u) r -> p c r u", u=PAIR),
             )
+            grouped_of[n] = grouped
 
-        def quantise(u):
-            codes = work.tile([P, TILES, PASSES, P], U32, name="codes", align_bytes=64)
-            scales = work.tile([P, TILES, PASSES, P], U8, name="scales", align_bytes=64)
+        def quantise(n):
+            codes = work.tile([P, PASSES, P], U32, name="codes", align_bytes=64)
+            scales = work.tile([P, PASSES, P], U8, name="scales", align_bytes=64)
             nc.vector.quantize_mx(
-                out=codes[:].rearrange("p j c r -> p (j c r)").bitcast(FP8X4),
-                scales=scales[:].rearrange("p j c r -> p (j c r)"),
-                in_=grouped_of[u][:].rearrange("p j c r t -> p (j c r t)"),
+                out=codes[:].rearrange("p c r -> p (c r)").bitcast(FP8X4),
+                scales=scales[:].rearrange("p c r -> p (c r)"),
+                in_=grouped_of[n][:].rearrange("p c r t -> p (c r t)"),
             )
-            codes_of[u] = codes
-            scales_of[u] = scales
+            codes_of[n] = codes
+            scales_of[n] = scales
 
         def project(n):
-            u, j = divmod(n, TILES)
             acc_of[n] = []
             for b in range(OUT_BANKS):
                 acc = psum_o.tile([P, PER_BANK, E], F32, name="acc%d" % b)
@@ -233,8 +217,8 @@ def tile_tinyblock_pa_t_kernel(
                 for c in range(PASSES):
                     nc.tensor.matmul_mx(
                         out=acc_of[n][i // PER_BANK][:, i % PER_BANK, :],
-                        lhsT=codes_of[u][:, j, c, :].bitcast(FP8X4),
-                        lhsT_scale=scales_of[u][:, j, c, :],
+                        lhsT=codes_of[n][:, c, :].bitcast(FP8X4),
+                        lhsT_scale=scales_of[n][:, c, :],
                         rhs=w_codes[:, i, c, :].bitcast(FP8X4),
                         rhs_scale=w_scales[:, i, c, :],
                         start=(c == 0),
@@ -266,17 +250,17 @@ def tile_tinyblock_pa_t_kernel(
 
         for n in range(LEAD):
             statistics(n)
-        for step in range(ALL_TILES + 4):
+        for step in range(ALL_TILES + 3):
             if 0 <= step - 1 < ALL_TILES:
                 copy_out(step - 1)
             if step + LEAD < ALL_TILES:
                 statistics(step + LEAD)
-            if 0 <= step - 3 < ALL_TILES:
-                project(step - 3)
+            if 0 <= step - 2 < ALL_TILES:
+                project(step - 2)
             if step < ALL_TILES:
                 normalise(step)
                 transpose(step)
-            if 0 <= step - 4 < ALL_TILES:
-                add_bias_and_store(step - 4)
-            if 0 <= step - 1 < ALL_TILES and (step - 1) % TILES == TILES - 1:
-                quantise((step - 1) // TILES)
+            if 0 <= step - 3 < ALL_TILES:
+                add_bias_and_store(step - 3)
+            if 0 <= step - 1 < ALL_TILES:
+                quantise(step - 1)

from contextlib import ExitStack

import concourse.mybir as mybir
from concourse.masks import make_identity

F32 = mybir.dt.float32
BF16 = mybir.dt.bfloat16
I32 = mybir.dt.int32
U32 = mybir.dt.uint32
U8 = mybir.dt.uint8
FP8X4 = mybir.dt.float8_e4m3fn_x4
ACT = mybir.ActivationFunctionType
ALU = mybir.AluOpType

P = 128
PACK = 4
PAIR = 2
K_PASS = P * PACK
TOKENS = 4 * 1024
D = 1024
E = 256
PROJ = 3
PASSES = D // K_PASS
HALVES = D // (P * PAIR)
TILES = 2
UNIT = TILES * P
UNITS = TOKENS // UNIT
ALL_TILES = TOKENS // P
BANK = 512
PER_BANK = BANK // E
OUT_BANKS = -(-PROJ // PER_BANK)
LEAD = 4
EPS = 1e-6

FLOPS = 2 * TOKENS * D * PROJ * E


def tile_tinyblock_pa_t_kernel(
    tc, x, attn_norm_w, wq, bq, wk, bk, wv, bv, out_0, out_1, out_2
):
    nc = tc.nc
    x_rows = x.flatten_outer_dims()
    out_rows = [out_0.flatten_outer_dims(), out_1.flatten_outer_dims(), out_2.flatten_outer_dims()]
    weights = [wq, wk, wv]
    biases = [bq, bk, bv]

    with ExitStack() as ctx:
        ctx.enter_context(tc.manual_schedule())
        const = ctx.enter_context(tc.tile_pool(name="const", bufs=1))
        x_pool = ctx.enter_context(tc.tile_pool(name="x", bufs=UNITS))
        small = ctx.enter_context(tc.tile_pool(name="small", bufs=LEAD + 2))
        normed = ctx.enter_context(tc.tile_pool(name="normed", bufs=LEAD + 2))
        work = ctx.enter_context(tc.tile_pool(name="work", bufs=3))
        store = ctx.enter_context(tc.tile_pool(name="store", bufs=3))
        psum_t = ctx.enter_context(tc.psum_pool(name="psum_t", bufs=4))
        psum_o = ctx.enter_context(tc.psum_pool(name="psum_o", bufs=2))

        vector_row = const.tile([1, D + PROJ * E], BF16)
        nc.sync.dma_start(out=vector_row[:, 0:D], in_=attn_norm_w.unsqueeze(0))
        for i in range(PROJ):
            nc.sync.dma_start(
                out=vector_row[:, D + i * E : D + (i + 1) * E], in_=biases[i].unsqueeze(0)
            )

        w_raw = const.tile([P, PROJ, PASSES * PACK, E], BF16)

        def load_weight(i):
            nc.sync.dma_start(
                out=w_raw[:, i].rearrange("p (h e) n -> p h (e n)", e=PAIR),
                in_=weights[i].rearrange("(h p e) n -> p h (e n)", p=P, e=PAIR),
            )

        x_units = []

        def load_unit(u):
            x_unit = x_pool.tile([P, TILES, D], BF16, name="x_unit")
            nc.sync.dma_start(
                out=x_unit[:],
                in_=x_rows[u * UNIT : (u + 1) * UNIT, :].rearrange("(p j) f -> p j f", j=TILES),
            )
            x_units.append(x_unit)

        load_weight(0)
        load_unit(0)
        for i in range(1, PROJ):
            load_weight(i)
        for u in range(1, UNITS):
            load_unit(u)

        eps = const.tile([P, 1], F32)
        nc.vector.memset(eps[:], EPS)
        vectors = const.tile([P, D + PROJ * E], BF16)
        nc.vector.memset(vectors[:].bitcast(I32), 0)
        nc.vector.tensor_copy(out=vectors[0:1, :], in_=vector_row[:])
        ones = const.tile([P, P], BF16)
        nc.vector.memset(ones[:], 1.0)
        ident = const.tile([P, P], F32)
        make_identity(nc, ident[:])

        warm = const.tile([P, 1], F32)
        nc.scalar.activation(out=warm[:], in_=eps[:], func=ACT.Abs_reciprocal_sqrt)

        gain = const.tile([P, D], BF16)
        bias = const.tile([P, PROJ, E], F32)
        for h in range(D // BANK):
            spread = psum_t.tile([P, BANK], F32, tag="xt")
            nc.tensor.matmul(
                out=spread[:], lhsT=ones[:], rhs=vectors[:, h * BANK : (h + 1) * BANK],
                start=True, stop=True,
            )
            nc.scalar.copy(out=gain[:, h * BANK : (h + 1) * BANK], in_=spread[:])
        for i in range(PROJ):
            spread = psum_t.tile([P, E], F32, tag="xt")
            nc.tensor.matmul(
                out=spread[:], lhsT=ones[:], rhs=vectors[:, D + i * E : D + (i + 1) * E],
                start=True, stop=True,
            )
            nc.scalar.copy(out=bias[:, i, :], in_=spread[:])

        w_grouped = const.tile([P, PROJ, PASSES, E, PACK], BF16, align_bytes=64)
        w_codes = const.tile([P, PROJ, PASSES, E], U32, align_bytes=64)
        w_scales = const.tile([P, PROJ, PASSES, E], U8, align_bytes=64)

        def group_weight(i):
            nc.vector.tensor_copy(
                out=w_grouped[:, i],
                in_=w_raw[:, i].rearrange("p (c t) n -> p c n t", t=PACK),
            )

        def quantise_weight(i):
            nc.vector.quantize_mx(
                out=w_codes[:, i].rearrange("p c n -> p (c n)").bitcast(FP8X4),
                scales=w_scales[:, i].rearrange("p c n -> p (c n)"),
                in_=w_grouped[:, i].rearrange("p c n t -> p (c n t)"),
            )

        group_weight(0)
        for i in range(1, PROJ):
            group_weight(i)
            quantise_weight(i - 1)
        quantise_weight(PROJ - 1)

        sumsq_of = {}
        rinv_of = {}
        xn_of = {}
        xt_of = {}
        grouped_of = {}
        codes_of = {}
        scales_of = {}
        acc_of = {}
        result_of = {}

        def statistics(n):
            u, j = divmod(n, TILES)
            if j == 0:
                sumsq = small.tile([P, TILES], F32, name="sumsq")
                sumsq_of[u] = sumsq
            squares = work.tile([P, D], BF16, name="squares")
            nc.scalar.activation(
                out=squares[:], in_=x_units[u][:, j, :], func=ACT.Square,
                accum_out=sumsq_of[u][:, j : j + 1],
            )
            if j == TILES - 1:
                rinv = small.tile([P, TILES], F32, name="rinv")
                nc.scalar.activation(
                    out=rinv[:], in_=sumsq_of[u][:], func=ACT.Abs_reciprocal_sqrt,
                    scale=1.0 / D, bias=eps[:],
                )
                rinv_of[u] = rinv

        def normalise(n):
            u, j = divmod(n, TILES)
            xn = normed.tile([P, D], BF16, name="xn")
            nc.vector.scalar_tensor_tensor(
                out=xn[:], in0=x_units[u][:, j, :], scalar=rinv_of[u][:, j : j + 1], in1=gain[:],
                op0=ALU.mult, op1=ALU.mult,
            )
            xn_of[n] = xn

        def transpose(n):
            xn_words = xn_of[n][:].bitcast(F32)
            xt = psum_t.tile([P, HALVES, P], F32, name="xt")
            for h in range(HALVES):
                nc.tensor.transpose(
                    out=xt[:, h, :], in_=xn_words[:, h * P : (h + 1) * P], identity=ident[:]
                )
            xt_of[n] = xt

        def copy_out(n):
            grouped = work.tile([P, PASSES, P, PACK], BF16, name="grouped", align_bytes=64)
            nc.scalar.copy(
                out=grouped[:]
                .rearrange("p c r t -> p (c r t)")
                .bitcast(F32)
                .rearrange("p (c r u) -> p c r u", c=PASSES, u=PAIR),
                in_=xt_of[n][:].rearrange("p (c u) r -> p c r u", u=PAIR),
            )
            grouped_of[n] = grouped

        def quantise(n):
            codes = work.tile([P, PASSES, P], U32, name="codes", align_bytes=64)
            scales = work.tile([P, PASSES, P], U8, name="scales", align_bytes=64)
            nc.vector.quantize_mx(
                out=codes[:].rearrange("p c r -> p (c r)").bitcast(FP8X4),
                scales=scales[:].rearrange("p c r -> p (c r)"),
                in_=grouped_of[n][:].rearrange("p c r t -> p (c r t)"),
            )
            codes_of[n] = codes
            scales_of[n] = scales

        def project(n):
            acc_of[n] = []
            for b in range(OUT_BANKS):
                acc = psum_o.tile([P, PER_BANK, E], F32, name="acc%d" % b)
                acc_of[n].append(acc)
            for i in range(PROJ):
                for c in range(PASSES):
                    nc.tensor.matmul_mx(
                        out=acc_of[n][i // PER_BANK][:, i % PER_BANK, :],
                        lhsT=codes_of[n][:, c, :].bitcast(FP8X4),
                        lhsT_scale=scales_of[n][:, c, :],
                        rhs=w_codes[:, i, c, :].bitcast(FP8X4),
                        rhs_scale=w_scales[:, i, c, :],
                        start=(c == 0),
                        stop=(c == PASSES - 1),
                    )

        def add_bias_and_store(n):
            u, j = divmod(n, TILES)
            if j == 0:
                result = store.tile([P, PROJ, TILES, E], F32, name="result")
                result_of[u] = result
            for b in range(OUT_BANKS):
                first = b * PER_BANK
                last = min(PROJ, first + PER_BANK)
                nc.vector.tensor_tensor(
                    out=result_of[u][:, first:last, j, :],
                    in0=acc_of[n][b][:, 0 : last - first, :],
                    in1=bias[:, first:last, :],
                    op=ALU.add,
                )
            if j == TILES - 1:
                for i in range(PROJ):
                    nc.sync.dma_start(
                        out=out_rows[i][u * UNIT : (u + 1) * UNIT, :].rearrange(
                            "(p j) e -> p j e", j=TILES
                        ),
                        in_=result_of[u][:, i],
                    )

        for n in range(LEAD):
            statistics(n)
        for step in range(ALL_TILES + 3):
            if 0 <= step - 1 < ALL_TILES:
                copy_out(step - 1)
            if step + LEAD < ALL_TILES:
                statistics(step + LEAD)
            if 0 <= step - 2 < ALL_TILES:
                project(step - 2)
            if step < ALL_TILES:
                normalise(step)
                transpose(step)
            if 0 <= step - 3 < ALL_TILES:
                add_bias_and_store(step - 3)
            if 0 <= step - 1 < ALL_TILES:
                quantise(step - 1)
